import numpy as np
import ml_dtypes

BF16 = ml_dtypes.bfloat16


def bf(x):
    return np.asarray(x, np.float32).astype(BF16)


def f32(x):
    return np.asarray(x, np.float32)


def f64(x):
    return np.asarray(x).astype(np.float64)


def striped(idx):
    return np.tile(idx.reshape(-1, 16).T, (8, 1))


C, S, N, K, D, F = 1024, 4096, 2048, 8, 128, 1024


def setup_inputs():
    return {
        "x": bf(np.random.standard_normal((F, N))),
        "w": bf(np.random.standard_normal((F, C)) / np.sqrt(F)),
        "bias": f32(np.random.uniform(-0.5, 0.5, (C, 1))),
        "base": f32(np.random.standard_normal((C, S))),
        "offs": striped(np.random.permutation(S)[:N]),
    }


def reference(x, w, bias, base, offs):
    idx = offs[:16].T.reshape(-1)
    xs = f64(x).reshape(K, D, N)
    ws = f64(w).reshape(K, D, C)
    y = np.zeros((C, N))
    for k in range(K):
        y = y + ws[k].T @ xs[k]
    out = f64(base).copy()
    out[:, idx] = y + f64(bias)
    return out

@@ -1,0 +1,69 @@
+import concourse.mybir as mybir
+
+BF16, F32, U16 = mybir.dt.bfloat16, mybir.dt.float32, mybir.dt.uint16
+
+P = 128
+C, S, N, K = 1024, 4096, 2048, 8
+BLOCKS = C // P
+BANK = 512
+PIECES = N // BANK
+
+FLOPS = 2 * C * (K * P) * N
+
+
+def tile_hkrpqlinear_b_kernel(tc, x, w, bias, base, offs, out):
+    nc = tc.nc
+    with (
+        tc.tile_pool(name="held", bufs=1) as held,
+        tc.tile_pool(name="sums", bufs=3) as sums,
+        tc.tile_pool(name="spread", bufs=2) as spread,
+        tc.psum_pool(name="banks", bufs=2) as banks,
+    ):
+        offsets = held.tile([P, N // 16], U16, name="offsets")
+        nc.sync.dma_start(offsets[:], offs)
+
+        bias_cols = held.tile([P, BLOCKS], F32, name="bias_cols")
+        with nc.allow_non_contiguous_dma(reason="1,024 single float32 values, once"):
+            nc.scalar.dma_start(bias_cols[:], bias.rearrange("(b p) o -> p (b o)", p=P))
+
+        w_books, x_books = [], []
+        for k in range(K):
+            w_book = held.tile([P, C], BF16, name=f"w_book{k}")
+            nc.sync.dma_start(w_book[:], w[k * P : (k + 1) * P, :])
+            w_books.append(w_book)
+            x_book = held.tile([P, N], BF16, name=f"x_book{k}")
+            nc.sync.dma_start(x_book[:], x[k * P : (k + 1) * P, :])
+            x_books.append(x_book)
+
+        windows = []
+        for b in range(BLOCKS):
+            window = held.tile([P, S], F32, name=f"window{b}")
+            nc.sync.dma_start(window[:], base[b * P : (b + 1) * P, :])
+            windows.append(window)
+
+        for b in range(BLOCKS):
+            bias_wide = spread.tile([P, N], F32, name="bias_wide")
+            nc.scalar.copy(bias_wide[:], bias_cols[:, b : b + 1].to_broadcast([P, N]))
+
+            acc = [banks.tile([P, BANK], F32, name=f"acc{n}") for n in range(PIECES)]
+            for k in range(K):
+                for n in range(PIECES):
+                    nc.tensor.matmul(
+                        acc[n][:],
+                        w_books[k][:, b * P : (b + 1) * P],
+                        x_books[k][:, n * BANK : (n + 1) * BANK],
+                        start=(k == 0),
+                        stop=(k == K - 1),
+                    )
+
+            y = sums.tile([P, N], F32, name="y")
+            for n in range(PIECES):
+                nc.scalar.copy(y[:, n * BANK : (n + 1) * BANK], acc[n][:])
+
+            nc.vector.tensor_tensor(
+                windows[b][:].indirect(offsets[:]),
+                y[:],
+                bias_wide[:],
+                mybir.AluOpType.add,
+            )
+            nc.sync.dma_start(out[b * P : (b + 1) * P, :], windows[b][:])

@@ -7,6 +7,7 @@ C, S, N, K = 1024, 4096, 2048, 8
 BLOCKS = C // P
 BANK = 512
 PIECES = N // BANK
+AHEAD = 4
 
 FLOPS = 2 * C * (K * P) * N
 
@@ -15,8 +16,8 @@ def tile_hkrpqlinear_b_kernel(tc, x, w, bias, base, offs, out):
     nc = tc.nc
     with (
         tc.tile_pool(name="held", bufs=1) as held,
+        tc.tile_pool(name="ring", bufs=AHEAD) as ring,
         tc.tile_pool(name="sums", bufs=3) as sums,
-        tc.tile_pool(name="spread", bufs=2) as spread,
         tc.psum_pool(name="banks", bufs=2) as banks,
     ):
         offsets = held.tile([P, N // 16], U16, name="offsets")
@@ -35,16 +36,23 @@ def tile_hkrpqlinear_b_kernel(tc, x, w, bias, base, offs, out):
             nc.sync.dma_start(x_book[:], x[k * P : (k + 1) * P, :])
             x_books.append(x_book)
 
-        windows = []
-        for b in range(BLOCKS):
-            window = held.tile([P, S], F32, name=f"window{b}")
+        def load_window(b):
+            window = ring.tile([P, S], F32, name="window")
             nc.sync.dma_start(window[:], base[b * P : (b + 1) * P, :])
-            windows.append(window)
+            return window
+
+        windows = [load_window(b) for b in range(AHEAD)]
+
+        bias_wide = []
+        for b in range(BLOCKS):
+            repeated = held.tile([P, N], F32, name=f"bias_wide{b}")
+            if b % 2 == 0:
+                nc.vector.tensor_copy(repeated[:], bias_cols[:, b : b + 1].to_broadcast([P, N]))
+            else:
+                nc.scalar.copy(repeated[:], bias_cols[:, b : b + 1].to_broadcast([P, N]))
+            bias_wide.append(repeated)
 
         for b in range(BLOCKS):
-            bias_wide = spread.tile([P, N], F32, name="bias_wide")
-            nc.scalar.copy(bias_wide[:], bias_cols[:, b : b + 1].to_broadcast([P, N]))
-
             acc = [banks.tile([P, BANK], F32, name=f"acc{n}") for n in range(PIECES)]
             for k in range(K):
                 for n in range(PIECES):
@@ -63,7 +71,9 @@ def tile_hkrpqlinear_b_kernel(tc, x, w, bias, base, offs, out):
             nc.vector.tensor_tensor(
                 windows[b][:].indirect(offsets[:]),
                 y[:],
-                bias_wide[:],
+                bias_wide[b][:],
                 mybir.AluOpType.add,
             )
             nc.sync.dma_start(out[b * P : (b + 1) * P, :], windows[b][:])
+            if b + AHEAD < BLOCKS:
+                windows.append(load_window(b + AHEAD))

@@ -27,21 +27,26 @@ def tile_hkrpqlinear_b_kernel(tc, x, w, bias, base, offs, out):
         with nc.allow_non_contiguous_dma(reason="1,024 single float32 values, once"):
             nc.scalar.dma_start(bias_cols[:], bias.rearrange("(b p) o -> p (b o)", p=P))
 
-        w_books, x_books = [], []
-        for k in range(K):
-            w_book = held.tile([P, C], BF16, name=f"w_book{k}")
-            nc.sync.dma_start(w_book[:], w[k * P : (k + 1) * P, :])
-            w_books.append(w_book)
-            x_book = held.tile([P, N], BF16, name=f"x_book{k}")
-            nc.sync.dma_start(x_book[:], x[k * P : (k + 1) * P, :])
-            x_books.append(x_book)
+        def load_words(b):
+            words = ring.tile([P, K, P], BF16, name="words")
+            nc.sync.dma_start(words[:], w[:, b * P : (b + 1) * P].rearrange("(k p) c -> p k c", p=P))
+            return words
 
         def load_window(b):
             window = ring.tile([P, S], F32, name="window")
             nc.sync.dma_start(window[:], base[b * P : (b + 1) * P, :])
             return window
 
-        windows = [load_window(b) for b in range(AHEAD)]
+        all_words = [load_words(0)]
+        x_books = []
+        for k in range(K):
+            x_book = held.tile([P, N], BF16, name=f"x_book{k}")
+            nc.sync.dma_start(x_book[:], x[k * P : (k + 1) * P, :])
+            x_books.append(x_book)
+        windows = [load_window(0)]
+        for b in range(1, AHEAD):
+            all_words.append(load_words(b))
+            windows.append(load_window(b))
 
         bias_wide = []
         for b in range(BLOCKS):
@@ -58,7 +63,7 @@ def tile_hkrpqlinear_b_kernel(tc, x, w, bias, base, offs, out):
                 for n in range(PIECES):
                     nc.tensor.matmul(
                         acc[n][:],
-                        w_books[k][:, b * P : (b + 1) * P],
+                        all_words[b][:, k, :],
                         x_books[k][:, n * BANK : (n + 1) * BANK],
                         start=(k == 0),
                         stop=(k == K - 1),
@@ -76,4 +81,5 @@ def tile_hkrpqlinear_b_kernel(tc, x, w, bias, base, offs, out):
             )
             nc.sync.dma_start(out[b * P : (b + 1) * P, :], windows[b][:])
             if b + AHEAD < BLOCKS:
+                all_words.append(load_words(b + AHEAD))
                 windows.append(load_window(b + AHEAD))

@@ -1,4 +1,5 @@
 import concourse.mybir as mybir
+from concourse.masks import make_identity
 
 BF16, F32, U16 = mybir.dt.bfloat16, mybir.dt.float32, mybir.dt.uint16
 
@@ -18,14 +19,20 @@ def tile_hkrpqlinear_b_kernel(tc, x, w, bias, base, offs, out):
         tc.tile_pool(name="held", bufs=1) as held,
         tc.tile_pool(name="ring", bufs=AHEAD) as ring,
         tc.tile_pool(name="sums", bufs=3) as sums,
-        tc.psum_pool(name="banks", bufs=2) as banks,
     ):
         offsets = held.tile([P, N // 16], U16, name="offsets")
         nc.sync.dma_start(offsets[:], offs)
 
+        bias_rows = held.tile([P, P], F32, name="bias_rows")
+        nc.vector.memset(bias_rows[:], 0.0)
+        nc.scalar.dma_start(bias_rows[0:BLOCKS, :], bias.rearrange("(b p) o -> b (p o)", p=P))
+        identity = held.tile([P, P], F32, name="identity")
+        make_identity(nc, identity[:])
         bias_cols = held.tile([P, BLOCKS], F32, name="bias_cols")
-        with nc.allow_non_contiguous_dma(reason="1,024 single float32 values, once"):
-            nc.scalar.dma_start(bias_cols[:], bias.rearrange("(b p) o -> p (b o)", p=P))
+        with tc.psum_pool(name="flip", bufs=1) as flip:
+            flipped = flip.tile([P, P], F32, name="flipped")
+            nc.tensor.transpose(flipped[:], bias_rows[:], identity[:])
+            nc.vector.tensor_copy(bias_cols[:], flipped[:, 0:BLOCKS])
 
         def load_words(b):
             words = ring.tile([P, K, P], BF16, name="words")
@@ -57,29 +64,30 @@ def tile_hkrpqlinear_b_kernel(tc, x, w, bias, base, offs, out):
                 nc.scalar.copy(repeated[:], bias_cols[:, b : b + 1].to_broadcast([P, N]))
             bias_wide.append(repeated)
 
-        for b in range(BLOCKS):
-            acc = [banks.tile([P, BANK], F32, name=f"acc{n}") for n in range(PIECES)]
-            for k in range(K):
+        with tc.psum_pool(name="banks", bufs=2) as banks:
+            for b in range(BLOCKS):
+                acc = [banks.tile([P, BANK], F32, name=f"acc{n}") for n in range(PIECES)]
+                for k in range(K):
+                    for n in range(PIECES):
+                        nc.tensor.matmul(
+                            acc[n][:],
+                            all_words[b][:, k, :],
+                            x_books[k][:, n * BANK : (n + 1) * BANK],
+                            start=(k == 0),
+                            stop=(k == K - 1),
+                        )
+
+                y = sums.tile([P, N], F32, name="y")
                 for n in range(PIECES):
-                    nc.tensor.matmul(
-                        acc[n][:],
-                        all_words[b][:, k, :],
-                        x_books[k][:, n * BANK : (n + 1) * BANK],
-                        start=(k == 0),
-                        stop=(k == K - 1),
-                    )
+                    nc.scalar.copy(y[:, n * BANK : (n + 1) * BANK], acc[n][:])
 
-            y = sums.tile([P, N], F32, name="y")
-            for n in range(PIECES):
-                nc.scalar.copy(y[:, n * BANK : (n + 1) * BANK], acc[n][:])
-
-            nc.vector.tensor_tensor(
-                windows[b][:].indirect(offsets[:]),
-                y[:],
-                bias_wide[b][:],
-                mybir.AluOpType.add,
-            )
-            nc.sync.dma_start(out[b * P : (b + 1) * P, :], windows[b][:])
-            if b + AHEAD < BLOCKS:
-                all_words.append(load_words(b + AHEAD))
-                windows.append(load_window(b + AHEAD))
+                nc.vector.tensor_tensor(
+                    windows[b][:].indirect(offsets[:]),
+                    y[:],
+                    bias_wide[b][:],
+                    mybir.AluOpType.add,
+                )
+                nc.sync.dma_start(out[b * P : (b + 1) * P, :], windows[b][:])
+                if b + AHEAD < BLOCKS:
+                    all_words.append(load_words(b + AHEAD))
+                    windows.append(load_window(b + AHEAD))

@@ -79,7 +79,11 @@ def tile_hkrpqlinear_b_kernel(tc, x, w, bias, base, offs, out):
 
                 y = sums.tile([P, N], F32, name="y")
                 for n in range(PIECES):
-                    nc.scalar.copy(y[:, n * BANK : (n + 1) * BANK], acc[n][:])
+                    part = y[:, n * BANK : (n + 1) * BANK]
+                    if b == 0 and n % 2 == 1:
+                        nc.vector.tensor_copy(part, acc[n][:])
+                    else:
+                        nc.scalar.copy(part, acc[n][:])
 
                 nc.vector.tensor_tensor(
                     windows[b][:].indirect(offsets[:]),

import concourse.mybir as mybir
from concourse.masks import make_identity

BF16, F32, U16 = mybir.dt.bfloat16, mybir.dt.float32, mybir.dt.uint16

P = 128
C, S, N, K = 1024, 4096, 2048, 8
BLOCKS = C // P
BANK = 512
PIECES = N // BANK
AHEAD = 4

FLOPS = 2 * C * (K * P) * N


def tile_hkrpqlinear_b_kernel(tc, x, w, bias, base, offs, out):
    nc = tc.nc
    with (
        tc.tile_pool(name="held", bufs=1) as held,
        tc.tile_pool(name="ring", bufs=AHEAD) as ring,
        tc.tile_pool(name="sums", bufs=3) as sums,
    ):
        offsets = held.tile([P, N // 16], U16, name="offsets")
        nc.sync.dma_start(offsets[:], offs)

        bias_rows = held.tile([P, P], F32, name="bias_rows")
        nc.vector.memset(bias_rows[:], 0.0)
        nc.scalar.dma_start(bias_rows[0:BLOCKS, :], bias.rearrange("(b p) o -> b (p o)", p=P))
        identity = held.tile([P, P], F32, name="identity")
        make_identity(nc, identity[:])
        bias_cols = held.tile([P, BLOCKS], F32, name="bias_cols")
        with tc.psum_pool(name="flip", bufs=1) as flip:
            flipped = flip.tile([P, P], F32, name="flipped")
            nc.tensor.transpose(flipped[:], bias_rows[:], identity[:])
            nc.vector.tensor_copy(bias_cols[:], flipped[:, 0:BLOCKS])

        def load_words(b):
            words = ring.tile([P, K, P], BF16, name="words")
            nc.sync.dma_start(words[:], w[:, b * P : (b + 1) * P].rearrange("(k p) c -> p k c", p=P))
            return words

        def load_window(b):
            window = ring.tile([P, S], F32, name="window")
            nc.sync.dma_start(window[:], base[b * P : (b + 1) * P, :])
            return window

        all_words = [load_words(0)]
        x_books = []
        for k in range(K):
            x_book = held.tile([P, N], BF16, name=f"x_book{k}")
            nc.sync.dma_start(x_book[:], x[k * P : (k + 1) * P, :])
            x_books.append(x_book)
        windows = [load_window(0)]
        for b in range(1, AHEAD):
            all_words.append(load_words(b))
            windows.append(load_window(b))

        bias_wide = []
        for b in range(BLOCKS):
            repeated = held.tile([P, N], F32, name=f"bias_wide{b}")
            if b % 2 == 0:
                nc.vector.tensor_copy(repeated[:], bias_cols[:, b : b + 1].to_broadcast([P, N]))
            else:
                nc.scalar.copy(repeated[:], bias_cols[:, b : b + 1].to_broadcast([P, N]))
            bias_wide.append(repeated)

        with tc.psum_pool(name="banks", bufs=2) as banks:
            for b in range(BLOCKS):
                acc = [banks.tile([P, BANK], F32, name=f"acc{n}") for n in range(PIECES)]
                for k in range(K):
                    for n in range(PIECES):
                        nc.tensor.matmul(
                            acc[n][:],
                            all_words[b][:, k, :],
                            x_books[k][:, n * BANK : (n + 1) * BANK],
                            start=(k == 0),
                            stop=(k == K - 1),
                        )

                y = sums.tile([P, N], F32, name="y")
                for n in range(PIECES):
                    part = y[:, n * BANK : (n + 1) * BANK]
                    if b == 0 and n % 2 == 1:
                        nc.vector.tensor_copy(part, acc[n][:])
                    else:
                        nc.scalar.copy(part, acc[n][:])

                nc.vector.tensor_tensor(
                    windows[b][:].indirect(offsets[:]),
                    y[:],
                    bias_wide[b][:],
                    mybir.AluOpType.add,
                )
                nc.sync.dma_start(out[b * P : (b + 1) * P, :], windows[b][:])
                if b + AHEAD < BLOCKS:
                    all_words.append(load_words(b + AHEAD))
                    windows.append(load_window(b + AHEAD))
